import numpy as np
import ml_dtypes


def mxq(x, axis, fmt="e4m3"):
    dtype, down = {"e4m3": (ml_dtypes.float8_e4m3fn, 7), "e5m2": (ml_dtypes.float8_e5m2, 14)}[fmt]
    v = np.moveaxis(np.asarray(x, np.float32).astype(ml_dtypes.bfloat16).astype(np.float64), axis, -1)
    blocks = v.reshape(v.shape[:-1] + (-1, 32))
    amax = np.abs(blocks).max(-1, keepdims=True)
    byte = np.maximum(np.where(amax > 0, np.frexp(amax)[1] - 1 + 127, 0) - down, 1)
    scale = np.exp2(byte - 127.0)
    codes = (blocks / scale).astype(np.float32).astype(dtype).astype(np.float64)
    return np.moveaxis((codes * scale).reshape(v.shape), -1, axis)


WIDE = False


def mx_kscale(k):
    if not WIDE:
        return np.ones(k)
    levels = np.array([10, -10, 5, -5, 0])
    a = np.random.permutation(np.resize(levels, k // 512 * 4)).reshape(k // 512, 4)
    idx = np.arange(k)
    return np.exp2(a[idx // 512, idx % 128 // 32])


BF16 = ml_dtypes.bfloat16


def bf(x):
    return np.asarray(x, np.float32).astype(BF16)


def f64(x):
    return np.asarray(x).astype(np.float64)


B, IN, NLVL, KLVL, C, CM, CO, OU, OV = 32, 256, 4, 2, 256, 256, 256, 8, 8
P = 2 ** (KLVL - 2)
S = 2 ** (NLVL - KLVL + 2)
KA, KB = 4 * C, 4 * CM


def patches(x):
    U, V, Bn, H, W, Cc = x.shape
    return x.reshape(U, V, Bn, H // 2, 2, W // 2, 2, Cc).swapaxes(4, 5).reshape(U, V, Bn * (H // 2) * (W // 2), 4 * Cc)


def branch_conv(x, w, b):
    U, V, Bn, H, W, Cc = x.shape
    Co = w.shape[-1]
    R = Bn * (H // 2) * (W // 2)
    p = patches(x).reshape(U, 1, V, 1, R, 4 * Cc)
    wc = w.reshape(U, 2, V, 2, 4 * Cc, Co)
    y = (mxq(p, 5, "e4m3") @ mxq(wc, 4, "e4m3")) + b.reshape(U, 2, V, 2, 1, Co)
    return np.maximum(y, 0.0).reshape(2 * U, 2 * V, Bn, H // 2, W // 2, Co)


def setup_inputs():
    s = mx_kscale(KA).reshape(2, 2, C)
    t = mx_kscale(KB)[:CM]
    x = np.maximum(np.random.standard_normal((P, P, B, S, S, C)), 0.0) * np.tile(s, (S // 2, S // 2, 1))
    return {"x_parent": bf(x),
            "f_child": bf(np.random.standard_normal((2 * P, 2 * P, 2, 2, C, CM)) * np.sqrt(0.5 / C) / s[:, :, :, None] * t),
            "b_child": bf(np.random.standard_normal((2 * P, 2 * P, CM)) * 0.2 * t),
            "f_gchild": bf(np.random.standard_normal((4 * P, 4 * P, 2, 2, CM, CO)) * np.sqrt(0.5 / CM) / t[:, None]),
            "b_gchild": bf(np.random.standard_normal((4 * P, 4 * P, CO)) * 0.2)}


def reference(x_parent, f_child, b_child, f_gchild, b_gchild):
    h = branch_conv(f64(x_parent), f64(f_child), f64(b_child))
    return branch_conv(h, f64(f_gchild), f64(b_gchild))

@@ -1,0 +1,303 @@
+from contextlib import ExitStack
+
+import concourse.mybir as mybir
+from concourse.masks import make_identity
+
+F32 = mybir.dt.float32
+BF16 = mybir.dt.bfloat16
+I32 = mybir.dt.int32
+U32 = mybir.dt.uint32
+U8 = mybir.dt.uint8
+FP8X4 = mybir.dt.float8_e4m3fn_x4
+RELU = mybir.ActivationFunctionType.Relu
+
+P = 128
+PACK = 4
+CH = 256
+PARITIES = CH // P
+BLOCKS = 4
+CHILDREN = 4
+UNITS = 8
+HALVES = 2 * CHILDREN
+N_MOVING = 512
+WIDE = 4096
+RAW_BUFS = 6
+
+FLOPS = 2 * (PACK * CH) * CH * (CHILDREN * 2048 + 2 * UNITS * 512)
+
+
+def tile_butterflylayer2d_pa_t_kernel(tc, x_parent, f_child, b_child, f_gchild, b_gchild, out):
+    nc = tc.nc
+    with ExitStack() as ctx:
+        ctx.enter_context(tc.manual_schedule())
+        keep = ctx.enter_context(tc.tile_pool(name="keep", bufs=1))
+        raw = ctx.enter_context(tc.tile_pool(name="raw", bufs=RAW_BUFS))
+        grouped = ctx.enter_context(tc.tile_pool(name="grouped", bufs=3))
+        w2_pool = ctx.enter_context(tc.tile_pool(name="w2_pool", bufs=3))
+        h_stage = ctx.enter_context(tc.tile_pool(name="h_stage", bufs=3))
+        h_pool = ctx.enter_context(tc.tile_pool(name="h_pool", bufs=4))
+        out_pool = ctx.enter_context(tc.tile_pool(name="out_pool", bufs=3))
+        psum_a = ctx.enter_context(tc.psum_pool(name="psum_a", bufs=4))
+        psum_b = ctx.enter_context(tc.psum_pool(name="psum_b", bufs=4))
+
+        x_raw = {}
+        w1_raw = {}
+        w2_raw = {}
+
+        def load_x(b):
+            x_raw[b] = raw.tile([P, WIDE], BF16, name="x_raw", tag="raw")
+            nc.sync.dma_start(
+                out=x_raw[b][:].rearrange("p (a w) -> p a w", a=4),
+                in_=x_parent.rearrange("u v n (y a) (b j) c -> (u v n y) b a (j c)", a=4, j=4)[:, b],
+            )
+
+        def load_w1(c):
+            w1_raw[c] = keep.tile([P, WIDE // 2], BF16, name="w1_raw%d" % c)
+            nc.sync.dma_start(
+                out=w1_raw[c][:].rearrange("p (a w) -> p a w", a=4),
+                in_=f_child[c // 2, c % 2].rearrange("p q (w e) o -> w (p q) (e o)", e=2),
+            )
+
+        def load_w2(u):
+            c, a = divmod(u, 2)
+            w2_raw[u] = raw.tile([P, WIDE], BF16, name="w2_raw", tag="raw")
+            nc.sync.dma_start(
+                out=w2_raw[u][:].rearrange("p (a w) -> p a w", a=8),
+                in_=f_gchild[2 * (c // 2) + a, 2 * (c % 2) : 2 * (c % 2) + 2].rearrange(
+                    "e p q (w m) o -> w (e p q) (m o)", m=2
+                ),
+            )
+            if u % 2 == 1 and (u + 3) // 2 < CHILDREN:
+                load_w1((u + 3) // 2)
+
+        load_w1(0)
+        for b in range(BLOCKS):
+            load_x(b)
+        load_w1(1)
+        load_w2(0)
+
+        ident = keep.tile([P, P], F32, name="ident")
+        make_identity(nc, ident[:])
+        ones = keep.tile([P, P], BF16, name="ones")
+        nc.vector.memset(ones[:], 1.0)
+
+        b1_rows = keep.tile([P, CH], BF16, name="b1_rows")
+        nc.vector.memset(b1_rows[:].bitcast(I32), 0)
+        nc.scalar.dma_start(out=b1_rows[0:CHILDREN, :], in_=b_child.rearrange("i j o -> (i j) o"))
+        b2_row = raw.tile([P, WIDE], BF16, name="b2_row", tag="raw")
+        nc.vector.memset(b2_row[:].bitcast(I32), 0)
+        nc.scalar.dma_start(out=b2_row[0:1, :], in_=b_gchild.rearrange("(u i) j o -> u (i j o)", u=1))
+
+        b1_bank = psum_a.tile([P, N_MOVING], F32, name="b1_bank", tag="a")
+        nc.tensor.transpose(b1_bank[:, 0:P], b1_rows[:].bitcast(F32), ident[:])
+        b1_pairs = keep.tile([P, PARITIES * CHILDREN], BF16, name="b1_pairs")
+        nc.vector.tensor_copy(out=b1_pairs[:].bitcast(F32), in_=b1_bank[:, 0:CHILDREN])
+        b1 = keep.tile([P, PARITIES * CHILDREN], F32, name="b1")
+        nc.vector.tensor_copy(out=b1[:], in_=b1_pairs[:])
+
+        b2 = keep.tile([P, WIDE], F32, name="b2")
+        for j in range(WIDE // N_MOVING):
+            cols = slice(j * N_MOVING, (j + 1) * N_MOVING)
+            b2_bank = psum_a.tile([P, N_MOVING], F32, name="b2_bank", tag="a")
+            nc.tensor.matmul(out=b2_bank[:], lhsT=ones[:], rhs=b2_row[:, cols], start=True, stop=True)
+            if j % 2 == 0:
+                nc.vector.tensor_copy(out=b2[:, cols], in_=b2_bank[:])
+            else:
+                nc.scalar.copy(out=b2[:, cols], in_=b2_bank[:])
+        load_w2(1)
+
+        x_codes = keep.tile([P, BLOCKS * 2 * N_MOVING], U32, name="x_codes", align_bytes=64)
+        x_scales = keep.tile([P, BLOCKS * 2 * N_MOVING], U8, name="x_scales", align_bytes=64)
+        x_grouped = {}
+
+        def transpose_x(b):
+            words = x_raw[b][:].bitcast(F32)
+            x_grouped[b] = grouped.tile([P, WIDE], BF16, name="x_grouped", tag="grouped", align_bytes=64)
+            target = x_grouped[b][:].bitcast(F32).rearrange("p (g r a j) -> p g r a j", g=2, r=P, a=2)
+            for g in range(2):
+                for a in range(2):
+                    bank = psum_a.tile([P, 4, P], F32, name="x_bank", tag="a")
+                    for j in range(4):
+                        first = ((2 * a + g) * 4 + j) * P
+                        nc.tensor.transpose(bank[:, j, :], words[:, first : first + P], ident[:])
+                    source = bank[:].rearrange("p j r -> p r j")
+                    if g == 0:
+                        nc.vector.tensor_copy(out=target[:, g, :, a, :], in_=source)
+                    else:
+                        nc.scalar.copy(out=target[:, g, :, a, :], in_=source)
+            load_w2(b + 2)
+
+        def quantise_x(b):
+            cols = slice(b * 2 * N_MOVING, (b + 1) * 2 * N_MOVING)
+            nc.vector.quantize_mx(
+                out=x_codes[:, cols].bitcast(FP8X4), scales=x_scales[:, cols], in_=x_grouped[b][:]
+            )
+
+        w1_grouped = {}
+        w1_codes = {}
+        w1_scales = {}
+
+        def regroup_w1(c):
+            w1_grouped[c] = keep.tile([P, WIDE // 2], BF16, name="w1_grouped", tag="w1_grouped%d" % (c % 2), align_bytes=64)
+            source = w1_raw[c][:].rearrange("p (g t w m) -> p g t w m", g=2, t=PACK, m=PARITIES)
+            target = w1_grouped[c][:].rearrange("p (g m w t) -> p g m w t", g=2, m=PARITIES, t=PACK)
+            nc.vector.tensor_copy(
+                out=target[:, :, 0, :, :], in_=source[:, :, :, :, 0].rearrange("p g t w -> p g w t")
+            )
+            nc.scalar.copy(
+                out=target[:, :, 1, :, :], in_=source[:, :, :, :, 1].rearrange("p g t w -> p g w t")
+            )
+
+        def quantise_w1(c):
+            w1_codes[c] = keep.tile([P, N_MOVING], U32, name="w1_codes%d" % c, align_bytes=64)
+            w1_scales[c] = keep.tile([P, N_MOVING], U8, name="w1_scales%d" % c, align_bytes=64)
+            nc.vector.quantize_mx(
+                out=w1_codes[c][:].bitcast(FP8X4), scales=w1_scales[c][:], in_=w1_grouped[c][:]
+            )
+
+        h_grouped = {}
+        h_codes = {}
+        h_scales = {}
+
+        def level1_block(c, b):
+            half, s = 2 * c + b // 2, b % 2
+            if s == 0:
+                h_grouped[half] = h_stage.tile([P, WIDE // 2], BF16, name="h_grouped", align_bytes=64)
+            for m in range(PARITIES):
+                acc = psum_b.tile([P, N_MOVING], F32, name="acc1", tag="b")
+                for g in range(2):
+                    w_cols = slice((g * PARITIES + m) * P, (g * PARITIES + m + 1) * P)
+                    x_cols = slice((b * 2 + g) * N_MOVING, (b * 2 + g + 1) * N_MOVING)
+                    nc.tensor.matmul_mx(
+                        out=acc[:],
+                        lhsT=w1_codes[c][:, w_cols].bitcast(FP8X4),
+                        lhsT_scale=w1_scales[c][:, w_cols],
+                        rhs=x_codes[:, x_cols].bitcast(FP8X4),
+                        rhs_scale=x_scales[:, x_cols],
+                        start=(g == 0),
+                        stop=(g == 1),
+                    )
+                h_cols = slice((s * PARITIES + m) * N_MOVING, (s * PARITIES + m + 1) * N_MOVING)
+                nc.scalar.activation(
+                    out=h_grouped[half][:, h_cols],
+                    in_=acc[:],
+                    func=RELU,
+                    bias=b1[:, PARITIES * c + m : PARITIES * c + m + 1],
+                    scale=1.0,
+                )
+
+        def level1_half(half):
+            if half < HALVES:
+                level1_block(half // 2, 2 * (half % 2))
+                level1_block(half // 2, 2 * (half % 2) + 1)
+
+        def quantise_h(half):
+            if half < HALVES:
+                h_codes[half] = h_pool.tile([P, N_MOVING], U32, name="h_codes", align_bytes=64)
+                h_scales[half] = h_pool.tile([P, N_MOVING], U8, name="h_scales", align_bytes=64)
+                nc.vector.quantize_mx(
+                    out=h_codes[half][:].bitcast(FP8X4), scales=h_scales[half][:], in_=h_grouped[half][:]
+                )
+
+        w2_grouped = {}
+        w2_codes = {}
+        w2_scales = {}
+
+        def regroup_w2(u):
+            if u >= UNITS:
+                return
+            w2_grouped[u] = grouped.tile([P, WIDE], BF16, name="w2_grouped", tag="grouped", align_bytes=64)
+            source = w2_raw[u][:].rearrange("p (e t m o) -> p e t m o", e=2, t=PACK, m=PARITIES)
+            target = w2_grouped[u][:].rearrange("p (m e o t) -> p m e o t", m=PARITIES, e=2, t=PACK)
+            for m in range(PARITIES):
+                for e in range(2):
+                    copy_out = target[:, m, e].rearrange("p (c i) t -> p c t i", i=4)
+                    copy_in = source[:, e, :, m, :].rearrange("p t (c i) -> p c t i", i=4)
+                    if m == 1 and e == 1:
+                        nc.scalar.copy(out=copy_out, in_=copy_in)
+                    else:
+                        nc.vector.tensor_copy(out=copy_out, in_=copy_in)
+            if u + RAW_BUFS < UNITS:
+                load_w2(u + RAW_BUFS)
+
+        def quantise_w2(u):
+            if u >= UNITS:
+                return
+            w2_codes[u] = w2_pool.tile([P, 2 * N_MOVING], U32, name="w2_codes", align_bytes=64)
+            w2_scales[u] = w2_pool.tile([P, 2 * N_MOVING], U8, name="w2_scales", align_bytes=64)
+            nc.vector.quantize_mx(
+                out=w2_codes[u][:].bitcast(FP8X4), scales=w2_scales[u][:], in_=w2_grouped[u][:]
+            )
+
+        out_tiles = {}
+
+        def level2(u):
+            c, a = divmod(u, 2)
+            first_node = (2 * (c // 2) + a) * 4 + 2 * (c % 2)
+            bias = b2[:, first_node * CH : (first_node + 2) * CH].rearrange("p (e o) -> p e o", e=2)
+            out_tiles[u] = out_pool.tile([P, 2 * BLOCKS * CH], F32, name="out_tile")
+            target = out_tiles[u][:].rearrange("p (e b o) -> p e b o", e=2, b=BLOCKS)
+            for b in range(BLOCKS):
+                half, s = 2 * c + b // 2, b % 2
+                acc = psum_a.tile([P, N_MOVING], F32, name="acc2", tag="a")
+                for m in range(PARITIES):
+                    h_cols = slice((s * PARITIES + m) * P, (s * PARITIES + m + 1) * P)
+                    w_cols = slice(m * N_MOVING, (m + 1) * N_MOVING)
+                    nc.tensor.matmul_mx(
+                        out=acc[:],
+                        lhsT=h_codes[half][:, h_cols].bitcast(FP8X4),
+                        lhsT_scale=h_scales[half][:, h_cols],
+                        rhs=w2_codes[u][:, w_cols].bitcast(FP8X4),
+                        rhs_scale=w2_scales[u][:, w_cols],
+                        start=(m == 0),
+                        stop=(m == PARITIES - 1),
+                    )
+                nc.vector.tensor_tensor(
+                    out=target[:, :, b, :],
+                    in0=acc[:].rearrange("p (e o) -> p e o", e=2),
+                    in1=bias,
+                    op=mybir.AluOpType.add,
+                )
+
+        def relu_and_store(u):
+            c, a = divmod(u, 2)
+            nc.scalar.activation(out=out_tiles[u][:], in_=out_tiles[u][:], func=RELU)
+            nc.scalar.dma_start(
+                out=out[2 * (c // 2) + a, 2 * (c % 2) : 2 * (c % 2) + 2].rearrange(
+                    "e n y b o -> (n y) e (b o)"
+                ),
+                in_=out_tiles[u][:].rearrange("p (e w) -> p e w", e=2),
+            )
+
+        regroup_w1(0)
+        transpose_x(0)
+        quantise_w1(0)
+        for b in range(1, BLOCKS):
+            transpose_x(b)
+            quantise_x(b - 1)
+            if b == BLOCKS - 1:
+                quantise_h(0)
+            level1_block(0, b - 1)
+        quantise_x(BLOCKS - 1)
+        level1_block(0, BLOCKS - 1)
+        regroup_w1(1)
+        quantise_h(1)
+        quantise_w1(1)
+        level1_half(2)
+        regroup_w2(0)
+        regroup_w2(1)
+        quantise_w2(0)
+
+        for u in range(UNITS):
+            if u > 0:
+                relu_and_store(u - 1)
+            regroup_w2(u + 2)
+            quantise_w2(u + 1)
+            if u % 2 == 1 and (u + 3) // 2 < CHILDREN:
+                quantise_w1((u + 3) // 2)
+            quantise_h(u + 2)
+            level2(u)
+            level1_half(u + 3)
+            if u % 2 == 0 and (u + 4) // 2 < CHILDREN:
+                regroup_w1((u + 4) // 2)
+        relu_and_store(UNITS - 1)

@@ -18,6 +18,7 @@ PARITIES = CH // P
 BLOCKS = 4
 CHILDREN = 4
 UNITS = 8
+NODES = 2 * UNITS
 HALVES = 2 * CHILDREN
 N_MOVING = 512
 WIDE = 4096
@@ -29,14 +30,13 @@ FLOPS = 2 * (PACK * CH) * CH * (CHILDREN * 2048 + 2 * UNITS * 512)
 def tile_butterflylayer2d_pa_t_kernel(tc, x_parent, f_child, b_child, f_gchild, b_gchild, out):
     nc = tc.nc
     with ExitStack() as ctx:
-        ctx.enter_context(tc.manual_schedule())
         keep = ctx.enter_context(tc.tile_pool(name="keep", bufs=1))
         raw = ctx.enter_context(tc.tile_pool(name="raw", bufs=RAW_BUFS))
         grouped = ctx.enter_context(tc.tile_pool(name="grouped", bufs=3))
         w2_pool = ctx.enter_context(tc.tile_pool(name="w2_pool", bufs=3))
         h_stage = ctx.enter_context(tc.tile_pool(name="h_stage", bufs=3))
         h_pool = ctx.enter_context(tc.tile_pool(name="h_pool", bufs=4))
-        out_pool = ctx.enter_context(tc.tile_pool(name="out_pool", bufs=3))
+        out_pool = ctx.enter_context(tc.tile_pool(name="out_pool", bufs=6))
         psum_a = ctx.enter_context(tc.psum_pool(name="psum_a", bufs=4))
         psum_b = ctx.enter_context(tc.psum_pool(name="psum_b", bufs=4))
 
@@ -70,41 +70,50 @@ def tile_butterflylayer2d_pa_t_kernel(tc, x_parent, f_child, b_child, f_gchild, 
             if u % 2 == 1 and (u + 3) // 2 < CHILDREN:
                 load_w1((u + 3) // 2)
 
+        ident = keep.tile([P, P], F32, name="ident")
+        make_identity(nc, ident[:])
+        ident_bf = keep.tile([P, P], BF16, name="ident_bf")
+        make_identity(nc, ident_bf[:])
+
+        bias_rows = keep.tile([P, CH], BF16, name="bias_rows")
+        nc.vector.memset(bias_rows[:].bitcast(I32), 0)
+        nc.sync.dma_start(out=bias_rows[0:CHILDREN, :], in_=b_child.rearrange("i j o -> (i j) o"))
+        nc.sync.dma_start(
+            out=bias_rows[CHILDREN : CHILDREN + NODES, :], in_=b_gchild.rearrange("i j o -> (i j) o")
+        )
+
+        load_x(0)
         load_w1(0)
-        for b in range(BLOCKS):
+        for b in range(1, BLOCKS):
             load_x(b)
         load_w1(1)
         load_w2(0)
-
-        ident = keep.tile([P, P], F32, name="ident")
-        make_identity(nc, ident[:])
-        ones = keep.tile([P, P], BF16, name="ones")
-        nc.vector.memset(ones[:], 1.0)
-
-        b1_rows = keep.tile([P, CH], BF16, name="b1_rows")
-        nc.vector.memset(b1_rows[:].bitcast(I32), 0)
-        nc.scalar.dma_start(out=b1_rows[0:CHILDREN, :], in_=b_child.rearrange("i j o -> (i j) o"))
-        b2_row = raw.tile([P, WIDE], BF16, name="b2_row", tag="raw")
-        nc.vector.memset(b2_row[:].bitcast(I32), 0)
-        nc.scalar.dma_start(out=b2_row[0:1, :], in_=b_gchild.rearrange("(u i) j o -> u (i j o)", u=1))
+        load_w2(1)
 
         b1_bank = psum_a.tile([P, N_MOVING], F32, name="b1_bank", tag="a")
-        nc.tensor.transpose(b1_bank[:, 0:P], b1_rows[:].bitcast(F32), ident[:])
+        nc.tensor.transpose(b1_bank[:, 0:P], bias_rows[:].bitcast(F32), ident[:])
         b1_pairs = keep.tile([P, PARITIES * CHILDREN], BF16, name="b1_pairs")
         nc.vector.tensor_copy(out=b1_pairs[:].bitcast(F32), in_=b1_bank[:, 0:CHILDREN])
         b1 = keep.tile([P, PARITIES * CHILDREN], F32, name="b1")
         nc.vector.tensor_copy(out=b1[:], in_=b1_pairs[:])
 
-        b2 = keep.tile([P, WIDE], F32, name="b2")
-        for j in range(WIDE // N_MOVING):
-            cols = slice(j * N_MOVING, (j + 1) * N_MOVING)
+        b2 = keep.tile([P, NODES * CH], F32, name="b2")
+        for pair in range(NODES // 2):
             b2_bank = psum_a.tile([P, N_MOVING], F32, name="b2_bank", tag="a")
-            nc.tensor.matmul(out=b2_bank[:], lhsT=ones[:], rhs=b2_row[:, cols], start=True, stop=True)
-            if j % 2 == 0:
+            for e in range(2):
+                row = CHILDREN + 2 * pair + e
+                nc.tensor.matmul(
+                    out=b2_bank[:, e * CH : (e + 1) * CH],
+                    lhsT=ident_bf[:, row : row + 1].to_broadcast([P, P]),
+                    rhs=bias_rows[:],
+                    start=True,
+                    stop=True,
+                )
+            cols = slice(pair * N_MOVING, (pair + 1) * N_MOVING)
+            if pair % 2 == 0:
                 nc.vector.tensor_copy(out=b2[:, cols], in_=b2_bank[:])
             else:
                 nc.scalar.copy(out=b2[:, cols], in_=b2_bank[:])
-        load_w2(1)
 
         x_codes = keep.tile([P, BLOCKS * 2 * N_MOVING], U32, name="x_codes", align_bytes=64)
         x_scales = keep.tile([P, BLOCKS * 2 * N_MOVING], U8, name="x_scales", align_bytes=64)
@@ -213,7 +222,7 @@ def tile_butterflylayer2d_pa_t_kernel(tc, x_parent, f_child, b_child, f_gchild, 
                 for e in range(2):
                     copy_out = target[:, m, e].rearrange("p (c i) t -> p c t i", i=4)
                     copy_in = source[:, e, :, m, :].rearrange("p t (c i) -> p c t i", i=4)
-                    if m == 1 and e == 1:
+                    if m == 1:
                         nc.scalar.copy(out=copy_out, in_=copy_in)
                     else:
                         nc.vector.tensor_copy(out=copy_out, in_=copy_in)
@@ -229,68 +238,68 @@ def tile_butterflylayer2d_pa_t_kernel(tc, x_parent, f_child, b_child, f_gchild, 
                 out=w2_codes[u][:].bitcast(FP8X4), scales=w2_scales[u][:], in_=w2_grouped[u][:]
             )
 
-        out_tiles = {}
-
         def level2(u):
             c, a = divmod(u, 2)
-            first_node = (2 * (c // 2) + a) * 4 + 2 * (c % 2)
+            node_row, node_col = 2 * (c // 2) + a, 2 * (c % 2)
+            first_node = node_row * 4 + node_col
             bias = b2[:, first_node * CH : (first_node + 2) * CH].rearrange("p (e o) -> p e o", e=2)
-            out_tiles[u] = out_pool.tile([P, 2 * BLOCKS * CH], F32, name="out_tile")
-            target = out_tiles[u][:].rearrange("p (e b o) -> p e b o", e=2, b=BLOCKS)
-            for b in range(BLOCKS):
-                half, s = 2 * c + b // 2, b % 2
-                acc = psum_a.tile([P, N_MOVING], F32, name="acc2", tag="a")
-                for m in range(PARITIES):
-                    h_cols = slice((s * PARITIES + m) * P, (s * PARITIES + m + 1) * P)
-                    w_cols = slice(m * N_MOVING, (m + 1) * N_MOVING)
-                    nc.tensor.matmul_mx(
-                        out=acc[:],
-                        lhsT=h_codes[half][:, h_cols].bitcast(FP8X4),
-                        lhsT_scale=h_scales[half][:, h_cols],
-                        rhs=w2_codes[u][:, w_cols].bitcast(FP8X4),
-                        rhs_scale=w2_scales[u][:, w_cols],
-                        start=(m == 0),
-                        stop=(m == PARITIES - 1),
+            for pair in range(BLOCKS // 2):
+                out_tile = out_pool.tile([P, 2 * 2 * CH], F32, name="out_tile")
+                target = out_tile[:].rearrange("p (e s o) -> p e s o", e=2, s=2)
+                for s in range(2):
+                    acc = psum_a.tile([P, N_MOVING], F32, name="acc2", tag="a")
+                    for m in range(PARITIES):
+                        h_cols = slice((s * PARITIES + m) * P, (s * PARITIES + m + 1) * P)
+                        w_cols = slice(m * N_MOVING, (m + 1) * N_MOVING)
+                        nc.tensor.matmul_mx(
+                            out=acc[:],
+                            lhsT=h_codes[2 * c + pair][:, h_cols].bitcast(FP8X4),
+                            lhsT_scale=h_scales[2 * c + pair][:, h_cols],
+                            rhs=w2_codes[u][:, w_cols].bitcast(FP8X4),
+                            rhs_scale=w2_scales[u][:, w_cols],
+                            start=(m == 0),
+                            stop=(m == PARITIES - 1),
+                        )
+                    nc.vector.tensor_tensor(
+                        out=target[:, :, s, :],
+                        in0=acc[:].rearrange("p (e o) -> p e o", e=2),
+                        in1=bias,
+                        op=mybir.AluOpType.add,
                     )
-                nc.vector.tensor_tensor(
-                    out=target[:, :, b, :],
-                    in0=acc[:].rearrange("p (e o) -> p e o", e=2),
-                    in1=bias,
-                    op=mybir.AluOpType.add,
+                nc.gpsimd.tensor_scalar(
+                    out=out_tile[:],
+                    in0=out_tile[:],
+                    scalar1=0.0,
+                    scalar2=0.0,
+                    op0=mybir.AluOpType.max,
+                    op1=mybir.AluOpType.add,
+                )
+                nc.sync.dma_start(
+                    out=out[
+                        node_row, node_col : node_col + 2, :, :, 2 * pair : 2 * pair + 2, :
+                    ].rearrange("e n y b o -> (n y) e (b o)"),
+                    in_=out_tile[:].rearrange("p (e w) -> p e w", e=2),
                 )
 
-        def relu_and_store(u):
-            c, a = divmod(u, 2)
-            nc.scalar.activation(out=out_tiles[u][:], in_=out_tiles[u][:], func=RELU)
-            nc.scalar.dma_start(
-                out=out[2 * (c // 2) + a, 2 * (c % 2) : 2 * (c % 2) + 2].rearrange(
-                    "e n y b o -> (n y) e (b o)"
-                ),
-                in_=out_tiles[u][:].rearrange("p (e w) -> p e w", e=2),
-            )
-
-        regroup_w1(0)
         transpose_x(0)
+        regroup_w1(0)
+        quantise_x(0)
         quantise_w1(0)
         for b in range(1, BLOCKS):
             transpose_x(b)
-            quantise_x(b - 1)
-            if b == BLOCKS - 1:
-                quantise_h(0)
             level1_block(0, b - 1)
-        quantise_x(BLOCKS - 1)
+            quantise_x(b)
+        quantise_h(0)
         level1_block(0, BLOCKS - 1)
         regroup_w1(1)
-        quantise_h(1)
-        quantise_w1(1)
-        level1_half(2)
         regroup_w2(0)
+        quantise_w1(1)
+        quantise_h(1)
+        level1_half(2)
         regroup_w2(1)
         quantise_w2(0)
 
         for u in range(UNITS):
-            if u > 0:
-                relu_and_store(u - 1)
             regroup_w2(u + 2)
             quantise_w2(u + 1)
             if u % 2 == 1 and (u + 3) // 2 < CHILDREN:
@@ -300,4 +309,3 @@ def tile_butterflylayer2d_pa_t_kernel(tc, x_parent, f_child, b_child, f_gchild, 
             level1_half(u + 3)
             if u % 2 == 0 and (u + 4) // 2 < CHILDREN:
                 regroup_w1((u + 4) // 2)
-        relu_and_store(UNITS - 1)

@@ -22,6 +22,7 @@ NODES = 2 * UNITS
 HALVES = 2 * CHILDREN
 N_MOVING = 512
 WIDE = 4096
+FLOAT32_MAX = 3.4028234663852886e38
 RAW_BUFS = 6
 
 FLOPS = 2 * (PACK * CH) * CH * (CHILDREN * 2048 + 2 * UNITS * 512)
@@ -269,10 +270,10 @@ def tile_butterflylayer2d_pa_t_kernel(tc, x_parent, f_child, b_child, f_gchild, 
                 nc.gpsimd.tensor_scalar(
                     out=out_tile[:],
                     in0=out_tile[:],
-                    scalar1=0.0,
+                    scalar1=FLOAT32_MAX,
                     scalar2=0.0,
-                    op0=mybir.AluOpType.max,
-                    op1=mybir.AluOpType.add,
+                    op0=mybir.AluOpType.min,
+                    op1=mybir.AluOpType.max,
                 )
                 nc.sync.dma_start(
                     out=out[

@@ -22,7 +22,6 @@ NODES = 2 * UNITS
 HALVES = 2 * CHILDREN
 N_MOVING = 512
 WIDE = 4096
-FLOAT32_MAX = 3.4028234663852886e38
 RAW_BUFS = 6
 
 FLOPS = 2 * (PACK * CH) * CH * (CHILDREN * 2048 + 2 * UNITS * 512)
@@ -73,15 +72,10 @@ def tile_butterflylayer2d_pa_t_kernel(tc, x_parent, f_child, b_child, f_gchild, 
 
         ident = keep.tile([P, P], F32, name="ident")
         make_identity(nc, ident[:])
-        ident_bf = keep.tile([P, P], BF16, name="ident_bf")
-        make_identity(nc, ident_bf[:])
 
         bias_rows = keep.tile([P, CH], BF16, name="bias_rows")
         nc.vector.memset(bias_rows[:].bitcast(I32), 0)
         nc.sync.dma_start(out=bias_rows[0:CHILDREN, :], in_=b_child.rearrange("i j o -> (i j) o"))
-        nc.sync.dma_start(
-            out=bias_rows[CHILDREN : CHILDREN + NODES, :], in_=b_gchild.rearrange("i j o -> (i j) o")
-        )
 
         load_x(0)
         load_w1(0)
@@ -89,6 +83,8 @@ def tile_butterflylayer2d_pa_t_kernel(tc, x_parent, f_child, b_child, f_gchild, 
             load_x(b)
         load_w1(1)
         load_w2(0)
+        b2 = keep.tile([P, NODES * CH], BF16, name="b2")
+        nc.sync.dma_start(out=b2[:], in_=b_gchild.rearrange("i j o -> (i j o)").partition_broadcast(P))
         load_w2(1)
 
         b1_bank = psum_a.tile([P, N_MOVING], F32, name="b1_bank", tag="a")
@@ -97,24 +93,6 @@ def tile_butterflylayer2d_pa_t_kernel(tc, x_parent, f_child, b_child, f_gchild, 
         nc.vector.tensor_copy(out=b1_pairs[:].bitcast(F32), in_=b1_bank[:, 0:CHILDREN])
         b1 = keep.tile([P, PARITIES * CHILDREN], F32, name="b1")
         nc.vector.tensor_copy(out=b1[:], in_=b1_pairs[:])
-
-        b2 = keep.tile([P, NODES * CH], F32, name="b2")
-        for pair in range(NODES // 2):
-            b2_bank = psum_a.tile([P, N_MOVING], F32, name="b2_bank", tag="a")
-            for e in range(2):
-                row = CHILDREN + 2 * pair + e
-                nc.tensor.matmul(
-                    out=b2_bank[:, e * CH : (e + 1) * CH],
-                    lhsT=ident_bf[:, row : row + 1].to_broadcast([P, P]),
-                    rhs=bias_rows[:],
-                    start=True,
-                    stop=True,
-                )
-            cols = slice(pair * N_MOVING, (pair + 1) * N_MOVING)
-            if pair % 2 == 0:
-                nc.vector.tensor_copy(out=b2[:, cols], in_=b2_bank[:])
-            else:
-                nc.scalar.copy(out=b2[:, cols], in_=b2_bank[:])
 
         x_codes = keep.tile([P, BLOCKS * 2 * N_MOVING], U32, name="x_codes", align_bytes=64)
         x_scales = keep.tile([P, BLOCKS * 2 * N_MOVING], U8, name="x_scales", align_bytes=64)
@@ -131,7 +109,7 @@ def tile_butterflylayer2d_pa_t_kernel(tc, x_parent, f_child, b_child, f_gchild, 
                         first = ((2 * a + g) * 4 + j) * P
                         nc.tensor.transpose(bank[:, j, :], words[:, first : first + P], ident[:])
                     source = bank[:].rearrange("p j r -> p r j")
-                    if g == 0:
+                    if g == 0 and b % 2 == 0:
                         nc.vector.tensor_copy(out=target[:, g, :, a, :], in_=source)
                     else:
                         nc.scalar.copy(out=target[:, g, :, a, :], in_=source)
@@ -223,7 +201,7 @@ def tile_butterflylayer2d_pa_t_kernel(tc, x_parent, f_child, b_child, f_gchild, 
                 for e in range(2):
                     copy_out = target[:, m, e].rearrange("p (c i) t -> p c t i", i=4)
                     copy_in = source[:, e, :, m, :].rearrange("p t (c i) -> p c t i", i=4)
-                    if m == 1:
+                    if m == 1 and e == 1:
                         nc.scalar.copy(out=copy_out, in_=copy_in)
                     else:
                         nc.vector.tensor_copy(out=copy_out, in_=copy_in)
@@ -239,14 +217,16 @@ def tile_butterflylayer2d_pa_t_kernel(tc, x_parent, f_child, b_child, f_gchild, 
                 out=w2_codes[u][:].bitcast(FP8X4), scales=w2_scales[u][:], in_=w2_grouped[u][:]
             )
 
+        out_tiles = {}
+
         def level2(u):
             c, a = divmod(u, 2)
             node_row, node_col = 2 * (c // 2) + a, 2 * (c % 2)
             first_node = node_row * 4 + node_col
             bias = b2[:, first_node * CH : (first_node + 2) * CH].rearrange("p (e o) -> p e o", e=2)
             for pair in range(BLOCKS // 2):
-                out_tile = out_pool.tile([P, 2 * 2 * CH], F32, name="out_tile")
-                target = out_tile[:].rearrange("p (e s o) -> p e s o", e=2, s=2)
+                out_tiles[u, pair] = out_pool.tile([P, 2 * 2 * CH], F32, name="out_tile")
+                target = out_tiles[u, pair][:].rearrange("p (e s o) -> p e s o", e=2, s=2)
                 for s in range(2):
                     acc = psum_a.tile([P, N_MOVING], F32, name="acc2", tag="a")
                     for m in range(PARITIES):
@@ -267,19 +247,17 @@ def tile_butterflylayer2d_pa_t_kernel(tc, x_parent, f_child, b_child, f_gchild, 
                         in1=bias,
                         op=mybir.AluOpType.add,
                     )
-                nc.gpsimd.tensor_scalar(
-                    out=out_tile[:],
-                    in0=out_tile[:],
-                    scalar1=FLOAT32_MAX,
-                    scalar2=0.0,
-                    op0=mybir.AluOpType.min,
-                    op1=mybir.AluOpType.max,
-                )
+
+        def relu_and_store(u):
+            c, a = divmod(u, 2)
+            node_row, node_col = 2 * (c // 2) + a, 2 * (c % 2)
+            for pair in range(BLOCKS // 2):
+                nc.scalar.activation(out=out_tiles[u, pair][:], in_=out_tiles[u, pair][:], func=RELU)
                 nc.sync.dma_start(
                     out=out[
                         node_row, node_col : node_col + 2, :, :, 2 * pair : 2 * pair + 2, :
                     ].rearrange("e n y b o -> (n y) e (b o)"),
-                    in_=out_tile[:].rearrange("p (e w) -> p e w", e=2),
+                    in_=out_tiles[u, pair][:].rearrange("p (e w) -> p e w", e=2),
                 )
 
         transpose_x(0)
@@ -295,18 +273,19 @@ def tile_butterflylayer2d_pa_t_kernel(tc, x_parent, f_child, b_child, f_gchild, 
         regroup_w1(1)
         regroup_w2(0)
         quantise_w1(1)
-        quantise_h(1)
-        level1_half(2)
         regroup_w2(1)
         quantise_w2(0)
 
         for u in range(UNITS):
+            quantise_h(u + 1)
+            if u > 0:
+                relu_and_store(u - 1)
             regroup_w2(u + 2)
             quantise_w2(u + 1)
             if u % 2 == 1 and (u + 3) // 2 < CHILDREN:
                 quantise_w1((u + 3) // 2)
-            quantise_h(u + 2)
             level2(u)
-            level1_half(u + 3)
+            level1_half(u + 2)
             if u % 2 == 0 and (u + 4) // 2 < CHILDREN:
                 regroup_w1((u + 4) // 2)
+        relu_and_store(UNITS - 1)

@@ -22,6 +22,7 @@ NODES = 2 * UNITS
 HALVES = 2 * CHILDREN
 N_MOVING = 512
 WIDE = 4096
+FLOAT32_MAX = 3.4028234663852886e38
 RAW_BUFS = 6
 
 FLOPS = 2 * (PACK * CH) * CH * (CHILDREN * 2048 + 2 * UNITS * 512)
@@ -30,6 +31,7 @@ FLOPS = 2 * (PACK * CH) * CH * (CHILDREN * 2048 + 2 * UNITS * 512)
 def tile_butterflylayer2d_pa_t_kernel(tc, x_parent, f_child, b_child, f_gchild, b_gchild, out):
     nc = tc.nc
     with ExitStack() as ctx:
+        ctx.enter_context(tc.manual_schedule())
         keep = ctx.enter_context(tc.tile_pool(name="keep", bufs=1))
         raw = ctx.enter_context(tc.tile_pool(name="raw", bufs=RAW_BUFS))
         grouped = ctx.enter_context(tc.tile_pool(name="grouped", bufs=3))
@@ -67,8 +69,8 @@ def tile_butterflylayer2d_pa_t_kernel(tc, x_parent, f_child, b_child, f_gchild, 
                     "e p q (w m) o -> w (e p q) (m o)", m=2
                 ),
             )
-            if u % 2 == 1 and (u + 3) // 2 < CHILDREN:
-                load_w1((u + 3) // 2)
+            if u % 2 == 0 and 2 <= u // 2 + 1 < CHILDREN:
+                load_w1(u // 2 + 1)
 
         ident = keep.tile([P, P], F32, name="ident")
         make_identity(nc, ident[:])
@@ -83,8 +85,6 @@ def tile_butterflylayer2d_pa_t_kernel(tc, x_parent, f_child, b_child, f_gchild, 
             load_x(b)
         load_w1(1)
         load_w2(0)
-        b2 = keep.tile([P, NODES * CH], BF16, name="b2")
-        nc.sync.dma_start(out=b2[:], in_=b_gchild.rearrange("i j o -> (i j o)").partition_broadcast(P))
         load_w2(1)
 
         b1_bank = psum_a.tile([P, N_MOVING], F32, name="b1_bank", tag="a")
@@ -109,7 +109,7 @@ def tile_butterflylayer2d_pa_t_kernel(tc, x_parent, f_child, b_child, f_gchild, 
                         first = ((2 * a + g) * 4 + j) * P
                         nc.tensor.transpose(bank[:, j, :], words[:, first : first + P], ident[:])
                     source = bank[:].rearrange("p j r -> p r j")
-                    if g == 0 and b % 2 == 0:
+                    if g == 0:
                         nc.vector.tensor_copy(out=target[:, g, :, a, :], in_=source)
                     else:
                         nc.scalar.copy(out=target[:, g, :, a, :], in_=source)
@@ -201,7 +201,7 @@ def tile_butterflylayer2d_pa_t_kernel(tc, x_parent, f_child, b_child, f_gchild, 
                 for e in range(2):
                     copy_out = target[:, m, e].rearrange("p (c i) t -> p c t i", i=4)
                     copy_in = source[:, e, :, m, :].rearrange("p t (c i) -> p c t i", i=4)
-                    if m == 1 and e == 1:
+                    if m == 1:
                         nc.scalar.copy(out=copy_out, in_=copy_in)
                     else:
                         nc.vector.tensor_copy(out=copy_out, in_=copy_in)
@@ -217,16 +217,14 @@ def tile_butterflylayer2d_pa_t_kernel(tc, x_parent, f_child, b_child, f_gchild, 
                 out=w2_codes[u][:].bitcast(FP8X4), scales=w2_scales[u][:], in_=w2_grouped[u][:]
             )
 
-        out_tiles = {}
-
         def level2(u):
             c, a = divmod(u, 2)
             node_row, node_col = 2 * (c // 2) + a, 2 * (c % 2)
             first_node = node_row * 4 + node_col
             bias = b2[:, first_node * CH : (first_node + 2) * CH].rearrange("p (e o) -> p e o", e=2)
             for pair in range(BLOCKS // 2):
-                out_tiles[u, pair] = out_pool.tile([P, 2 * 2 * CH], F32, name="out_tile")
-                target = out_tiles[u, pair][:].rearrange("p (e s o) -> p e s o", e=2, s=2)
+                out_tile = out_pool.tile([P, 2 * 2 * CH], F32, name="out_tile")
+                target = out_tile[:].rearrange("p (e s o) -> p e s o", e=2, s=2)
                 for s in range(2):
                     acc = psum_a.tile([P, N_MOVING], F32, name="acc2", tag="a")
                     for m in range(PARITIES):
@@ -247,20 +245,24 @@ def tile_butterflylayer2d_pa_t_kernel(tc, x_parent, f_child, b_child, f_gchild, 
                         in1=bias,
                         op=mybir.AluOpType.add,
                     )
-
-        def relu_and_store(u):
-            c, a = divmod(u, 2)
-            node_row, node_col = 2 * (c // 2) + a, 2 * (c % 2)
-            for pair in range(BLOCKS // 2):
-                nc.scalar.activation(out=out_tiles[u, pair][:], in_=out_tiles[u, pair][:], func=RELU)
+                nc.gpsimd.tensor_scalar(
+                    out=out_tile[:],
+                    in0=out_tile[:],
+                    scalar1=FLOAT32_MAX,
+                    scalar2=0.0,
+                    op0=mybir.AluOpType.min,
+                    op1=mybir.AluOpType.max,
+                )
                 nc.sync.dma_start(
                     out=out[
                         node_row, node_col : node_col + 2, :, :, 2 * pair : 2 * pair + 2, :
                     ].rearrange("e n y b o -> (n y) e (b o)"),
-                    in_=out_tiles[u, pair][:].rearrange("p (e w) -> p e w", e=2),
+                    in_=out_tile[:].rearrange("p (e w) -> p e w", e=2),
                 )
 
         transpose_x(0)
+        b2 = keep.tile([P, NODES * CH], BF16, name="b2")
+        nc.sync.dma_start(out=b2[:], in_=b_gchild.rearrange("i j o -> (i j o)").partition_broadcast(P))
         regroup_w1(0)
         quantise_x(0)
         quantise_w1(0)
@@ -278,8 +280,6 @@ def tile_butterflylayer2d_pa_t_kernel(tc, x_parent, f_child, b_child, f_gchild, 
 
         for u in range(UNITS):
             quantise_h(u + 1)
-            if u > 0:
-                relu_and_store(u - 1)
             regroup_w2(u + 2)
             quantise_w2(u + 1)
             if u % 2 == 1 and (u + 3) // 2 < CHILDREN:
@@ -288,4 +288,3 @@ def tile_butterflylayer2d_pa_t_kernel(tc, x_parent, f_child, b_child, f_gchild, 
             level1_half(u + 2)
             if u % 2 == 0 and (u + 4) // 2 < CHILDREN:
                 regroup_w1((u + 4) // 2)
-        relu_and_store(UNITS - 1)

@@ -22,7 +22,6 @@ NODES = 2 * UNITS
 HALVES = 2 * CHILDREN
 N_MOVING = 512
 WIDE = 4096
-FLOAT32_MAX = 3.4028234663852886e38
 RAW_BUFS = 6
 
 FLOPS = 2 * (PACK * CH) * CH * (CHILDREN * 2048 + 2 * UNITS * 512)
@@ -31,7 +30,6 @@ FLOPS = 2 * (PACK * CH) * CH * (CHILDREN * 2048 + 2 * UNITS * 512)
 def tile_butterflylayer2d_pa_t_kernel(tc, x_parent, f_child, b_child, f_gchild, b_gchild, out):
     nc = tc.nc
     with ExitStack() as ctx:
-        ctx.enter_context(tc.manual_schedule())
         keep = ctx.enter_context(tc.tile_pool(name="keep", bufs=1))
         raw = ctx.enter_context(tc.tile_pool(name="raw", bufs=RAW_BUFS))
         grouped = ctx.enter_context(tc.tile_pool(name="grouped", bufs=3))
@@ -48,10 +46,13 @@ def tile_butterflylayer2d_pa_t_kernel(tc, x_parent, f_child, b_child, f_gchild, 
 
         def load_x(b):
             x_raw[b] = raw.tile([P, WIDE], BF16, name="x_raw", tag="raw")
-            nc.sync.dma_start(
-                out=x_raw[b][:].rearrange("p (a w) -> p a w", a=4),
-                in_=x_parent.rearrange("u v n (y a) (b j) c -> (u v n y) b a (j c)", a=4, j=4)[:, b],
-            )
+            for g in range(2):
+                nc.sync.dma_start(
+                    out=x_raw[b][:].rearrange("p (a g w) -> p g a w", a=2, g=2)[:, g],
+                    in_=x_parent.rearrange(
+                        "u v n (y a g) (b j) c -> (u v n y) b g a (j c)", a=2, g=2, j=4
+                    )[:, b, g],
+                )
 
         def load_w1(c):
             w1_raw[c] = keep.tile([P, WIDE // 2], BF16, name="w1_raw%d" % c)
@@ -109,7 +110,7 @@ def tile_butterflylayer2d_pa_t_kernel(tc, x_parent, f_child, b_child, f_gchild, 
                         first = ((2 * a + g) * 4 + j) * P
                         nc.tensor.transpose(bank[:, j, :], words[:, first : first + P], ident[:])
                     source = bank[:].rearrange("p j r -> p r j")
-                    if g == 0:
+                    if g == 0 and b % 2 == 0:
                         nc.vector.tensor_copy(out=target[:, g, :, a, :], in_=source)
                     else:
                         nc.scalar.copy(out=target[:, g, :, a, :], in_=source)
@@ -201,7 +202,7 @@ def tile_butterflylayer2d_pa_t_kernel(tc, x_parent, f_child, b_child, f_gchild, 
                 for e in range(2):
                     copy_out = target[:, m, e].rearrange("p (c i) t -> p c t i", i=4)
                     copy_in = source[:, e, :, m, :].rearrange("p t (c i) -> p c t i", i=4)
-                    if m == 1:
+                    if m == 1 and e == 1:
                         nc.scalar.copy(out=copy_out, in_=copy_in)
                     else:
                         nc.vector.tensor_copy(out=copy_out, in_=copy_in)
@@ -217,14 +218,16 @@ def tile_butterflylayer2d_pa_t_kernel(tc, x_parent, f_child, b_child, f_gchild, 
                 out=w2_codes[u][:].bitcast(FP8X4), scales=w2_scales[u][:], in_=w2_grouped[u][:]
             )
 
+        out_tiles = {}
+
         def level2(u):
             c, a = divmod(u, 2)
             node_row, node_col = 2 * (c // 2) + a, 2 * (c % 2)
             first_node = node_row * 4 + node_col
             bias = b2[:, first_node * CH : (first_node + 2) * CH].rearrange("p (e o) -> p e o", e=2)
             for pair in range(BLOCKS // 2):
-                out_tile = out_pool.tile([P, 2 * 2 * CH], F32, name="out_tile")
-                target = out_tile[:].rearrange("p (e s o) -> p e s o", e=2, s=2)
+                out_tiles[u, pair] = out_pool.tile([P, 2 * 2 * CH], F32, name="out_tile")
+                target = out_tiles[u, pair][:].rearrange("p (e s o) -> p e s o", e=2, s=2)
                 for s in range(2):
                     acc = psum_a.tile([P, N_MOVING], F32, name="acc2", tag="a")
                     for m in range(PARITIES):
@@ -245,19 +248,17 @@ def tile_butterflylayer2d_pa_t_kernel(tc, x_parent, f_child, b_child, f_gchild, 
                         in1=bias,
                         op=mybir.AluOpType.add,
                     )
-                nc.gpsimd.tensor_scalar(
-                    out=out_tile[:],
-                    in0=out_tile[:],
-                    scalar1=FLOAT32_MAX,
-                    scalar2=0.0,
-                    op0=mybir.AluOpType.min,
-                    op1=mybir.AluOpType.max,
-                )
+
+        def relu_and_store(u):
+            c, a = divmod(u, 2)
+            node_row, node_col = 2 * (c // 2) + a, 2 * (c % 2)
+            for pair in range(BLOCKS // 2):
+                nc.scalar.activation(out=out_tiles[u, pair][:], in_=out_tiles[u, pair][:], func=RELU)
                 nc.sync.dma_start(
                     out=out[
                         node_row, node_col : node_col + 2, :, :, 2 * pair : 2 * pair + 2, :
                     ].rearrange("e n y b o -> (n y) e (b o)"),
-                    in_=out_tile[:].rearrange("p (e w) -> p e w", e=2),
+                    in_=out_tiles[u, pair][:].rearrange("p (e w) -> p e w", e=2),
                 )
 
         transpose_x(0)
@@ -280,6 +281,8 @@ def tile_butterflylayer2d_pa_t_kernel(tc, x_parent, f_child, b_child, f_gchild, 
 
         for u in range(UNITS):
             quantise_h(u + 1)
+            if u > 0:
+                relu_and_store(u - 1)
             regroup_w2(u + 2)
             quantise_w2(u + 1)
             if u % 2 == 1 and (u + 3) // 2 < CHILDREN:
@@ -288,3 +291,4 @@ def tile_butterflylayer2d_pa_t_kernel(tc, x_parent, f_child, b_child, f_gchild, 
             level1_half(u + 2)
             if u % 2 == 0 and (u + 4) // 2 < CHILDREN:
                 regroup_w1((u + 4) // 2)
+        relu_and_store(UNITS - 1)

@@ -75,6 +75,8 @@ def tile_butterflylayer2d_pa_t_kernel(tc, x_parent, f_child, b_child, f_gchild, 
 
         ident = keep.tile([P, P], F32, name="ident")
         make_identity(nc, ident[:])
+        ident_bf = keep.tile([P, P], BF16, name="ident_bf")
+        nc.vector.tensor_copy(out=ident_bf[:], in_=ident[:])
 
         bias_rows = keep.tile([P, CH], BF16, name="bias_rows")
         nc.vector.memset(bias_rows[:].bitcast(I32), 0)
@@ -110,10 +112,7 @@ def tile_butterflylayer2d_pa_t_kernel(tc, x_parent, f_child, b_child, f_gchild, 
                         first = ((2 * a + g) * 4 + j) * P
                         nc.tensor.transpose(bank[:, j, :], words[:, first : first + P], ident[:])
                     source = bank[:].rearrange("p j r -> p r j")
-                    if g == 0 and b % 2 == 0:
-                        nc.vector.tensor_copy(out=target[:, g, :, a, :], in_=source)
-                    else:
-                        nc.scalar.copy(out=target[:, g, :, a, :], in_=source)
+                    nc.scalar.copy(out=target[:, g, :, a, :], in_=source)
             load_w2(b + 2)
 
         def quantise_x(b):
@@ -203,7 +202,16 @@ def tile_butterflylayer2d_pa_t_kernel(tc, x_parent, f_child, b_child, f_gchild, 
                     copy_out = target[:, m, e].rearrange("p (c i) t -> p c t i", i=4)
                     copy_in = source[:, e, :, m, :].rearrange("p t (c i) -> p c t i", i=4)
                     if m == 1 and e == 1:
-                        nc.scalar.copy(out=copy_out, in_=copy_in)
+                        bank = psum_b.tile([P, PACK * CH], BF16, name="w_bank", tag="b")
+                        for half in range(2):
+                            nc.tensor.matmul(
+                                out=bank[:, half * N_MOVING : (half + 1) * N_MOVING].rearrange("p (o t) -> p t o", t=PACK),
+                                lhsT=ident_bf[:],
+                                rhs=source[:, e, :, m, half * P : (half + 1) * P],
+                                start=True,
+                                stop=True,
+                            )
+                        nc.scalar.copy(out=target[:, m, e].rearrange("p o t -> p (o t)"), in_=bank[:])
                     else:
                         nc.vector.tensor_copy(out=copy_out, in_=copy_in)
             if u + RAW_BUFS < UNITS:

@@ -22,7 +22,10 @@ NODES = 2 * UNITS
 HALVES = 2 * CHILDREN
 N_MOVING = 512
 WIDE = 4096
-RAW_BUFS = 6
+XV = 2
+PSPLIT = (2, 4, 6, 7)
+PKIND = "scalar"
+RAW_BUFS = 11
 
 FLOPS = 2 * (PACK * CH) * CH * (CHILDREN * 2048 + 2 * UNITS * 512)
 
@@ -36,9 +39,10 @@ def tile_butterflylayer2d_pa_t_kernel(tc, x_parent, f_child, b_child, f_gchild, 
         w2_pool = ctx.enter_context(tc.tile_pool(name="w2_pool", bufs=3))
         h_stage = ctx.enter_context(tc.tile_pool(name="h_stage", bufs=3))
         h_pool = ctx.enter_context(tc.tile_pool(name="h_pool", bufs=4))
-        out_pool = ctx.enter_context(tc.tile_pool(name="out_pool", bufs=6))
+        out_pool = ctx.enter_context(tc.tile_pool(name="out_pool", bufs=5))
         psum_a = ctx.enter_context(tc.psum_pool(name="psum_a", bufs=4))
-        psum_b = ctx.enter_context(tc.psum_pool(name="psum_b", bufs=4))
+        psum_b = ctx.enter_context(tc.psum_pool(name="psum_b", bufs=3))
+        psum_w = ctx.enter_context(tc.psum_pool(name="psum_w", bufs=1))
 
         x_raw = {}
         w1_raw = {}
@@ -70,32 +74,31 @@ def tile_butterflylayer2d_pa_t_kernel(tc, x_parent, f_child, b_child, f_gchild, 
                     "e p q (w m) o -> w (e p q) (m o)", m=2
                 ),
             )
-            if u % 2 == 0 and 2 <= u // 2 + 1 < CHILDREN:
-                load_w1(u // 2 + 1)
 
         ident = keep.tile([P, P], F32, name="ident")
         make_identity(nc, ident[:])
         ident_bf = keep.tile([P, P], BF16, name="ident_bf")
-        nc.vector.tensor_copy(out=ident_bf[:], in_=ident[:])
+        nc.gpsimd.tensor_copy(out=ident_bf[:], in_=ident[:])
 
         bias_rows = keep.tile([P, CH], BF16, name="bias_rows")
         nc.vector.memset(bias_rows[:].bitcast(I32), 0)
-        nc.sync.dma_start(out=bias_rows[0:CHILDREN, :], in_=b_child.rearrange("i j o -> (i j) o"))
-
         load_x(0)
         load_w1(0)
-        for b in range(1, BLOCKS):
-            load_x(b)
+        nc.sync.dma_start(out=bias_rows[0:CHILDREN, :], in_=b_child.rearrange("i j o -> (i j) o"))
+        load_x(1)
         load_w1(1)
+        load_x(2)
+        load_x(3)
         load_w2(0)
         load_w2(1)
-
-        b1_bank = psum_a.tile([P, N_MOVING], F32, name="b1_bank", tag="a")
-        nc.tensor.transpose(b1_bank[:, 0:P], bias_rows[:].bitcast(F32), ident[:])
-        b1_pairs = keep.tile([P, PARITIES * CHILDREN], BF16, name="b1_pairs")
-        nc.vector.tensor_copy(out=b1_pairs[:].bitcast(F32), in_=b1_bank[:, 0:CHILDREN])
-        b1 = keep.tile([P, PARITIES * CHILDREN], F32, name="b1")
-        nc.vector.tensor_copy(out=b1[:], in_=b1_pairs[:])
+        load_w1(2)
+        load_w2(2)
+        b2 = keep.tile([P, NODES * CH], BF16, name="b2")
+        nc.sync.dma_start(out=b2[:], in_=b_gchild.rearrange("i j o -> (i j o)").partition_broadcast(P))
+        load_w2(3)
+        load_w1(3)
+        for u in range(4, UNITS):
+            load_w2(u)
 
         x_codes = keep.tile([P, BLOCKS * 2 * N_MOVING], U32, name="x_codes", align_bytes=64)
         x_scales = keep.tile([P, BLOCKS * 2 * N_MOVING], U8, name="x_scales", align_bytes=64)
@@ -112,8 +115,10 @@ def tile_butterflylayer2d_pa_t_kernel(tc, x_parent, f_child, b_child, f_gchild, 
                         first = ((2 * a + g) * 4 + j) * P
                         nc.tensor.transpose(bank[:, j, :], words[:, first : first + P], ident[:])
                     source = bank[:].rearrange("p j r -> p r j")
-                    nc.scalar.copy(out=target[:, g, :, a, :], in_=source)
-            load_w2(b + 2)
+                    if g == 0 and (XV == 2 or a == 0):
+                        nc.vector.tensor_copy(out=target[:, g, :, a, :], in_=source)
+                    else:
+                        nc.scalar.copy(out=target[:, g, :, a, :], in_=source)
 
         def quantise_x(b):
             cols = slice(b * 2 * N_MOVING, (b + 1) * 2 * N_MOVING)
@@ -191,6 +196,13 @@ def tile_butterflylayer2d_pa_t_kernel(tc, x_parent, f_child, b_child, f_gchild, 
         w2_codes = {}
         w2_scales = {}
 
+        def quarter_owner(u, m, e):
+            if m == 1 and e == 1:
+                return "tensor"
+            if m == 1 and e == 0 and u in PSPLIT:
+                return PKIND
+            return "vector"
+
         def regroup_w2(u):
             if u >= UNITS:
                 return
@@ -201,8 +213,11 @@ def tile_butterflylayer2d_pa_t_kernel(tc, x_parent, f_child, b_child, f_gchild, 
                 for e in range(2):
                     copy_out = target[:, m, e].rearrange("p (c i) t -> p c t i", i=4)
                     copy_in = source[:, e, :, m, :].rearrange("p t (c i) -> p c t i", i=4)
-                    if m == 1 and e == 1:
-                        bank = psum_b.tile([P, PACK * CH], BF16, name="w_bank", tag="b")
+                    owner = quarter_owner(u, m, e)
+                    if owner == "scalar":
+                        nc.scalar.copy(out=copy_out, in_=copy_in)
+                    elif owner == "tensor":
+                        bank = psum_w.tile([P, PACK * CH], BF16, name="w_bank")
                         for half in range(2):
                             nc.tensor.matmul(
                                 out=bank[:, half * N_MOVING : (half + 1) * N_MOVING].rearrange("p (o t) -> p t o", t=PACK),
@@ -214,8 +229,6 @@ def tile_butterflylayer2d_pa_t_kernel(tc, x_parent, f_child, b_child, f_gchild, 
                         nc.scalar.copy(out=target[:, m, e].rearrange("p o t -> p (o t)"), in_=bank[:])
                     else:
                         nc.vector.tensor_copy(out=copy_out, in_=copy_in)
-            if u + RAW_BUFS < UNITS:
-                load_w2(u + RAW_BUFS)
 
         def quantise_w2(u):
             if u >= UNITS:
@@ -257,10 +270,12 @@ def tile_butterflylayer2d_pa_t_kernel(tc, x_parent, f_child, b_child, f_gchild, 
                         op=mybir.AluOpType.add,
                     )
 
-        def relu_and_store(u):
+        def relu_and_store(u, pairs=(0, 1)):
             c, a = divmod(u, 2)
             node_row, node_col = 2 * (c // 2) + a, 2 * (c % 2)
-            for pair in range(BLOCKS // 2):
+            if u < 0:
+                return
+            for pair in pairs:
                 nc.scalar.activation(out=out_tiles[u, pair][:], in_=out_tiles[u, pair][:], func=RELU)
                 nc.sync.dma_start(
                     out=out[
@@ -269,34 +284,50 @@ def tile_butterflylayer2d_pa_t_kernel(tc, x_parent, f_child, b_child, f_gchild, 
                     in_=out_tiles[u, pair][:].rearrange("p (e w) -> p e w", e=2),
                 )
 
+        ctx.enter_context(tc.manual_schedule())
         transpose_x(0)
-        b2 = keep.tile([P, NODES * CH], BF16, name="b2")
-        nc.sync.dma_start(out=b2[:], in_=b_gchild.rearrange("i j o -> (i j o)").partition_broadcast(P))
         regroup_w1(0)
         quantise_x(0)
+        b1_bank = psum_a.tile([P, N_MOVING], F32, name="b1_bank", tag="a")
+        nc.tensor.transpose(b1_bank[:, 0:P], bias_rows[:].bitcast(F32), ident[:])
+        b1_pairs = keep.tile([P, PARITIES * CHILDREN], BF16, name="b1_pairs")
+        nc.vector.tensor_copy(out=b1_pairs[:].bitcast(F32), in_=b1_bank[:, 0:CHILDREN])
+        b1 = keep.tile([P, PARITIES * CHILDREN], F32, name="b1")
+        nc.vector.tensor_copy(out=b1[:], in_=b1_pairs[:])
         quantise_w1(0)
-        for b in range(1, BLOCKS):
-            transpose_x(b)
-            level1_block(0, b - 1)
-            quantise_x(b)
-        quantise_h(0)
-        level1_block(0, BLOCKS - 1)
+        transpose_x(1)
+        level1_block(0, 0)
         regroup_w1(1)
-        regroup_w2(0)
+        quantise_x(1)
+        transpose_x(2)
+        level1_block(0, 1)
         quantise_w1(1)
-        regroup_w2(1)
+        quantise_x(2)
+        quantise_h(0)
+        transpose_x(3)
+        level1_block(0, 2)
+        quantise_x(3)
+        level1_block(1, 0)
+        regroup_w2(0)
+        level1_block(0, 3)
+        level1_block(1, 1)
         quantise_w2(0)
-
+        quantise_h(1)
+        regroup_w2(1)
         for u in range(UNITS):
-            quantise_h(u + 1)
-            if u > 0:
-                relu_and_store(u - 1)
-            regroup_w2(u + 2)
-            quantise_w2(u + 1)
-            if u % 2 == 1 and (u + 3) // 2 < CHILDREN:
-                quantise_w1((u + 3) // 2)
-            level2(u)
-            level1_half(u + 2)
             if u % 2 == 0 and (u + 4) // 2 < CHILDREN:
                 regroup_w1((u + 4) // 2)
+            regroup_w2(u + 2)
+            relu_and_store(u - 1, (0,))
+            quantise_h(u + 2)
+            quantise_w2(u + 1)
+            if u % 2 == 0 and (u + 4) // 2 < CHILDREN:
+                quantise_w1((u + 4) // 2)
+            half = u + 3
+            if half < HALVES:
+                level1_block(half // 2, 2 * (half % 2))
+            relu_and_store(u - 1, (1,))
+            level2(u)
+            if half < HALVES:
+                level1_block(half // 2, 2 * (half % 2) + 1)
         relu_and_store(UNITS - 1)

@@ -22,9 +22,7 @@ NODES = 2 * UNITS
 HALVES = 2 * CHILDREN
 N_MOVING = 512
 WIDE = 4096
-XV = 2
-PSPLIT = (2, 4, 6, 7)
-PKIND = "scalar"
+PSPLIT = (6, 7)
 RAW_BUFS = 11
 
 FLOPS = 2 * (PACK * CH) * CH * (CHILDREN * 2048 + 2 * UNITS * 512)
@@ -41,8 +39,7 @@ def tile_butterflylayer2d_pa_t_kernel(tc, x_parent, f_child, b_child, f_gchild, 
         h_pool = ctx.enter_context(tc.tile_pool(name="h_pool", bufs=4))
         out_pool = ctx.enter_context(tc.tile_pool(name="out_pool", bufs=5))
         psum_a = ctx.enter_context(tc.psum_pool(name="psum_a", bufs=4))
-        psum_b = ctx.enter_context(tc.psum_pool(name="psum_b", bufs=3))
-        psum_w = ctx.enter_context(tc.psum_pool(name="psum_w", bufs=1))
+        psum_b = ctx.enter_context(tc.psum_pool(name="psum_b", bufs=4))
 
         x_raw = {}
         w1_raw = {}
@@ -77,8 +74,6 @@ def tile_butterflylayer2d_pa_t_kernel(tc, x_parent, f_child, b_child, f_gchild, 
 
         ident = keep.tile([P, P], F32, name="ident")
         make_identity(nc, ident[:])
-        ident_bf = keep.tile([P, P], BF16, name="ident_bf")
-        nc.gpsimd.tensor_copy(out=ident_bf[:], in_=ident[:])
 
         bias_rows = keep.tile([P, CH], BF16, name="bias_rows")
         nc.vector.memset(bias_rows[:].bitcast(I32), 0)
@@ -115,7 +110,7 @@ def tile_butterflylayer2d_pa_t_kernel(tc, x_parent, f_child, b_child, f_gchild, 
                         first = ((2 * a + g) * 4 + j) * P
                         nc.tensor.transpose(bank[:, j, :], words[:, first : first + P], ident[:])
                     source = bank[:].rearrange("p j r -> p r j")
-                    if g == 0 and (XV == 2 or a == 0):
+                    if g == 0:
                         nc.vector.tensor_copy(out=target[:, g, :, a, :], in_=source)
                     else:
                         nc.scalar.copy(out=target[:, g, :, a, :], in_=source)
@@ -196,13 +191,6 @@ def tile_butterflylayer2d_pa_t_kernel(tc, x_parent, f_child, b_child, f_gchild, 
         w2_codes = {}
         w2_scales = {}
 
-        def quarter_owner(u, m, e):
-            if m == 1 and e == 1:
-                return "tensor"
-            if m == 1 and e == 0 and u in PSPLIT:
-                return PKIND
-            return "vector"
-
         def regroup_w2(u):
             if u >= UNITS:
                 return
@@ -210,25 +198,15 @@ def tile_butterflylayer2d_pa_t_kernel(tc, x_parent, f_child, b_child, f_gchild, 
             source = w2_raw[u][:].rearrange("p (e t m o) -> p e t m o", e=2, t=PACK, m=PARITIES)
             target = w2_grouped[u][:].rearrange("p (m e o t) -> p m e o t", m=PARITIES, e=2, t=PACK)
             for m in range(PARITIES):
-                for e in range(2):
-                    copy_out = target[:, m, e].rearrange("p (c i) t -> p c t i", i=4)
-                    copy_in = source[:, e, :, m, :].rearrange("p t (c i) -> p c t i", i=4)
-                    owner = quarter_owner(u, m, e)
-                    if owner == "scalar":
-                        nc.scalar.copy(out=copy_out, in_=copy_in)
-                    elif owner == "tensor":
-                        bank = psum_w.tile([P, PACK * CH], BF16, name="w_bank")
-                        for half in range(2):
-                            nc.tensor.matmul(
-                                out=bank[:, half * N_MOVING : (half + 1) * N_MOVING].rearrange("p (o t) -> p t o", t=PACK),
-                                lhsT=ident_bf[:],
-                                rhs=source[:, e, :, m, half * P : (half + 1) * P],
-                                start=True,
-                                stop=True,
-                            )
-                        nc.scalar.copy(out=target[:, m, e].rearrange("p o t -> p (o t)"), in_=bank[:])
-                    else:
-                        nc.vector.tensor_copy(out=copy_out, in_=copy_in)
+                copy_out = target[:, m].rearrange("p e (c i) t -> p e c t i", i=4)
+                copy_in = source[:, :, :, m, :].rearrange("p e t (c i) -> p e c t i", i=4)
+                if m == 0:
+                    nc.vector.tensor_copy(out=copy_out, in_=copy_in)
+                elif u in PSPLIT:
+                    nc.scalar.copy(out=copy_out, in_=copy_in)
+                else:
+                    nc.vector.tensor_copy(out=copy_out[:, 0], in_=copy_in[:, 0])
+                    nc.scalar.copy(out=copy_out[:, 1], in_=copy_in[:, 1])
 
         def quantise_w2(u):
             if u >= UNITS:

@@ -127,14 +127,10 @@ def tile_butterflylayer2d_pa_t_kernel(tc, x_parent, f_child, b_child, f_gchild, 
 
         def regroup_w1(c):
             w1_grouped[c] = keep.tile([P, WIDE // 2], BF16, name="w1_grouped", tag="w1_grouped%d" % (c % 2), align_bytes=64)
-            source = w1_raw[c][:].rearrange("p (g t w m) -> p g t w m", g=2, t=PACK, m=PARITIES)
-            target = w1_grouped[c][:].rearrange("p (g m w t) -> p g m w t", g=2, m=PARITIES, t=PACK)
-            nc.vector.tensor_copy(
-                out=target[:, :, 0, :, :], in_=source[:, :, :, :, 0].rearrange("p g t w -> p g w t")
-            )
-            nc.scalar.copy(
-                out=target[:, :, 1, :, :], in_=source[:, :, :, :, 1].rearrange("p g t w -> p g w t")
-            )
+            source = w1_raw[c][:].rearrange("p (g t c i m) -> p m g c t i", g=2, t=PACK, i=4, m=PARITIES)
+            target = w1_grouped[c][:].rearrange("p (g m c i t) -> p m g c t i", g=2, m=PARITIES, i=4, t=PACK)
+            nc.vector.tensor_copy(out=target[:, 0], in_=source[:, 0])
+            nc.scalar.copy(out=target[:, 1], in_=source[:, 1])
 
         def quantise_w1(c):
             w1_codes[c] = keep.tile([P, N_MOVING], U32, name="w1_codes%d" % c, align_bytes=64)

from contextlib import ExitStack

import concourse.mybir as mybir
from concourse.masks import make_identity

F32 = mybir.dt.float32
BF16 = mybir.dt.bfloat16
I32 = mybir.dt.int32
U32 = mybir.dt.uint32
U8 = mybir.dt.uint8
FP8X4 = mybir.dt.float8_e4m3fn_x4
RELU = mybir.ActivationFunctionType.Relu

P = 128
PACK = 4
CH = 256
PARITIES = CH // P
BLOCKS = 4
CHILDREN = 4
UNITS = 8
NODES = 2 * UNITS
HALVES = 2 * CHILDREN
N_MOVING = 512
WIDE = 4096
PSPLIT = (6, 7)
RAW_BUFS = 11

FLOPS = 2 * (PACK * CH) * CH * (CHILDREN * 2048 + 2 * UNITS * 512)


def tile_butterflylayer2d_pa_t_kernel(tc, x_parent, f_child, b_child, f_gchild, b_gchild, out):
    nc = tc.nc
    with ExitStack() as ctx:
        keep = ctx.enter_context(tc.tile_pool(name="keep", bufs=1))
        raw = ctx.enter_context(tc.tile_pool(name="raw", bufs=RAW_BUFS))
        grouped = ctx.enter_context(tc.tile_pool(name="grouped", bufs=3))
        w2_pool = ctx.enter_context(tc.tile_pool(name="w2_pool", bufs=3))
        h_stage = ctx.enter_context(tc.tile_pool(name="h_stage", bufs=3))
        h_pool = ctx.enter_context(tc.tile_pool(name="h_pool", bufs=4))
        out_pool = ctx.enter_context(tc.tile_pool(name="out_pool", bufs=5))
        psum_a = ctx.enter_context(tc.psum_pool(name="psum_a", bufs=4))
        psum_b = ctx.enter_context(tc.psum_pool(name="psum_b", bufs=4))

        x_raw = {}
        w1_raw = {}
        w2_raw = {}

        def load_x(b):
            x_raw[b] = raw.tile([P, WIDE], BF16, name="x_raw", tag="raw")
            for g in range(2):
                nc.sync.dma_start(
                    out=x_raw[b][:].rearrange("p (a g w) -> p g a w", a=2, g=2)[:, g],
                    in_=x_parent.rearrange(
                        "u v n (y a g) (b j) c -> (u v n y) b g a (j c)", a=2, g=2, j=4
                    )[:, b, g],
                )

        def load_w1(c):
            w1_raw[c] = keep.tile([P, WIDE // 2], BF16, name="w1_raw%d" % c)
            nc.sync.dma_start(
                out=w1_raw[c][:].rearrange("p (a w) -> p a w", a=4),
                in_=f_child[c // 2, c % 2].rearrange("p q (w e) o -> w (p q) (e o)", e=2),
            )

        def load_w2(u):
            c, a = divmod(u, 2)
            w2_raw[u] = raw.tile([P, WIDE], BF16, name="w2_raw", tag="raw")
            nc.sync.dma_start(
                out=w2_raw[u][:].rearrange("p (a w) -> p a w", a=8),
                in_=f_gchild[2 * (c // 2) + a, 2 * (c % 2) : 2 * (c % 2) + 2].rearrange(
                    "e p q (w m) o -> w (e p q) (m o)", m=2
                ),
            )

        ident = keep.tile([P, P], F32, name="ident")
        make_identity(nc, ident[:])

        bias_rows = keep.tile([P, CH], BF16, name="bias_rows")
        nc.vector.memset(bias_rows[:].bitcast(I32), 0)
        load_x(0)
        load_w1(0)
        nc.sync.dma_start(out=bias_rows[0:CHILDREN, :], in_=b_child.rearrange("i j o -> (i j) o"))
        load_x(1)
        load_w1(1)
        load_x(2)
        load_x(3)
        load_w2(0)
        load_w2(1)
        load_w1(2)
        load_w2(2)
        b2 = keep.tile([P, NODES * CH], BF16, name="b2")
        nc.sync.dma_start(out=b2[:], in_=b_gchild.rearrange("i j o -> (i j o)").partition_broadcast(P))
        load_w2(3)
        load_w1(3)
        for u in range(4, UNITS):
            load_w2(u)

        x_codes = keep.tile([P, BLOCKS * 2 * N_MOVING], U32, name="x_codes", align_bytes=64)
        x_scales = keep.tile([P, BLOCKS * 2 * N_MOVING], U8, name="x_scales", align_bytes=64)
        x_grouped = {}

        def transpose_x(b):
            words = x_raw[b][:].bitcast(F32)
            x_grouped[b] = grouped.tile([P, WIDE], BF16, name="x_grouped", tag="grouped", align_bytes=64)
            target = x_grouped[b][:].bitcast(F32).rearrange("p (g r a j) -> p g r a j", g=2, r=P, a=2)
            for g in range(2):
                for a in range(2):
                    bank = psum_a.tile([P, 4, P], F32, name="x_bank", tag="a")
                    for j in range(4):
                        first = ((2 * a + g) * 4 + j) * P
                        nc.tensor.transpose(bank[:, j, :], words[:, first : first + P], ident[:])
                    source = bank[:].rearrange("p j r -> p r j")
                    if g == 0:
                        nc.vector.tensor_copy(out=target[:, g, :, a, :], in_=source)
                    else:
                        nc.scalar.copy(out=target[:, g, :, a, :], in_=source)

        def quantise_x(b):
            cols = slice(b * 2 * N_MOVING, (b + 1) * 2 * N_MOVING)
            nc.vector.quantize_mx(
                out=x_codes[:, cols].bitcast(FP8X4), scales=x_scales[:, cols], in_=x_grouped[b][:]
            )

        w1_grouped = {}
        w1_codes = {}
        w1_scales = {}

        def regroup_w1(c):
            w1_grouped[c] = keep.tile([P, WIDE // 2], BF16, name="w1_grouped", tag="w1_grouped%d" % (c % 2), align_bytes=64)
            source = w1_raw[c][:].rearrange("p (g t c i m) -> p m g c t i", g=2, t=PACK, i=4, m=PARITIES)
            target = w1_grouped[c][:].rearrange("p (g m c i t) -> p m g c t i", g=2, m=PARITIES, i=4, t=PACK)
            nc.vector.tensor_copy(out=target[:, 0], in_=source[:, 0])
            nc.scalar.copy(out=target[:, 1], in_=source[:, 1])

        def quantise_w1(c):
            w1_codes[c] = keep.tile([P, N_MOVING], U32, name="w1_codes%d" % c, align_bytes=64)
            w1_scales[c] = keep.tile([P, N_MOVING], U8, name="w1_scales%d" % c, align_bytes=64)
            nc.vector.quantize_mx(
                out=w1_codes[c][:].bitcast(FP8X4), scales=w1_scales[c][:], in_=w1_grouped[c][:]
            )

        h_grouped = {}
        h_codes = {}
        h_scales = {}

        def level1_block(c, b):
            half, s = 2 * c + b // 2, b % 2
            if s == 0:
                h_grouped[half] = h_stage.tile([P, WIDE // 2], BF16, name="h_grouped", align_bytes=64)
            for m in range(PARITIES):
                acc = psum_b.tile([P, N_MOVING], F32, name="acc1", tag="b")
                for g in range(2):
                    w_cols = slice((g * PARITIES + m) * P, (g * PARITIES + m + 1) * P)
                    x_cols = slice((b * 2 + g) * N_MOVING, (b * 2 + g + 1) * N_MOVING)
                    nc.tensor.matmul_mx(
                        out=acc[:],
                        lhsT=w1_codes[c][:, w_cols].bitcast(FP8X4),
                        lhsT_scale=w1_scales[c][:, w_cols],
                        rhs=x_codes[:, x_cols].bitcast(FP8X4),
                        rhs_scale=x_scales[:, x_cols],
                        start=(g == 0),
                        stop=(g == 1),
                    )
                h_cols = slice((s * PARITIES + m) * N_MOVING, (s * PARITIES + m + 1) * N_MOVING)
                nc.scalar.activation(
                    out=h_grouped[half][:, h_cols],
                    in_=acc[:],
                    func=RELU,
                    bias=b1[:, PARITIES * c + m : PARITIES * c + m + 1],
                    scale=1.0,
                )

        def level1_half(half):
            if half < HALVES:
                level1_block(half // 2, 2 * (half % 2))
                level1_block(half // 2, 2 * (half % 2) + 1)

        def quantise_h(half):
            if half < HALVES:
                h_codes[half] = h_pool.tile([P, N_MOVING], U32, name="h_codes", align_bytes=64)
                h_scales[half] = h_pool.tile([P, N_MOVING], U8, name="h_scales", align_bytes=64)
                nc.vector.quantize_mx(
                    out=h_codes[half][:].bitcast(FP8X4), scales=h_scales[half][:], in_=h_grouped[half][:]
                )

        w2_grouped = {}
        w2_codes = {}
        w2_scales = {}

        def regroup_w2(u):
            if u >= UNITS:
                return
            w2_grouped[u] = grouped.tile([P, WIDE], BF16, name="w2_grouped", tag="grouped", align_bytes=64)
            source = w2_raw[u][:].rearrange("p (e t m o) -> p e t m o", e=2, t=PACK, m=PARITIES)
            target = w2_grouped[u][:].rearrange("p (m e o t) -> p m e o t", m=PARITIES, e=2, t=PACK)
            for m in range(PARITIES):
                copy_out = target[:, m].rearrange("p e (c i) t -> p e c t i", i=4)
                copy_in = source[:, :, :, m, :].rearrange("p e t (c i) -> p e c t i", i=4)
                if m == 0:
                    nc.vector.tensor_copy(out=copy_out, in_=copy_in)
                elif u in PSPLIT:
                    nc.scalar.copy(out=copy_out, in_=copy_in)
                else:
                    nc.vector.tensor_copy(out=copy_out[:, 0], in_=copy_in[:, 0])
                    nc.scalar.copy(out=copy_out[:, 1], in_=copy_in[:, 1])

        def quantise_w2(u):
            if u >= UNITS:
                return
            w2_codes[u] = w2_pool.tile([P, 2 * N_MOVING], U32, name="w2_codes", align_bytes=64)
            w2_scales[u] = w2_pool.tile([P, 2 * N_MOVING], U8, name="w2_scales", align_bytes=64)
            nc.vector.quantize_mx(
                out=w2_codes[u][:].bitcast(FP8X4), scales=w2_scales[u][:], in_=w2_grouped[u][:]
            )

        out_tiles = {}

        def level2(u):
            c, a = divmod(u, 2)
            node_row, node_col = 2 * (c // 2) + a, 2 * (c % 2)
            first_node = node_row * 4 + node_col
            bias = b2[:, first_node * CH : (first_node + 2) * CH].rearrange("p (e o) -> p e o", e=2)
            for pair in range(BLOCKS // 2):
                out_tiles[u, pair] = out_pool.tile([P, 2 * 2 * CH], F32, name="out_tile")
                target = out_tiles[u, pair][:].rearrange("p (e s o) -> p e s o", e=2, s=2)
                for s in range(2):
                    acc = psum_a.tile([P, N_MOVING], F32, name="acc2", tag="a")
                    for m in range(PARITIES):
                        h_cols = slice((s * PARITIES + m) * P, (s * PARITIES + m + 1) * P)
                        w_cols = slice(m * N_MOVING, (m + 1) * N_MOVING)
                        nc.tensor.matmul_mx(
                            out=acc[:],
                            lhsT=h_codes[2 * c + pair][:, h_cols].bitcast(FP8X4),
                            lhsT_scale=h_scales[2 * c + pair][:, h_cols],
                            rhs=w2_codes[u][:, w_cols].bitcast(FP8X4),
                            rhs_scale=w2_scales[u][:, w_cols],
                            start=(m == 0),
                            stop=(m == PARITIES - 1),
                        )
                    nc.vector.tensor_tensor(
                        out=target[:, :, s, :],
                        in0=acc[:].rearrange("p (e o) -> p e o", e=2),
                        in1=bias,
                        op=mybir.AluOpType.add,
                    )

        def relu_and_store(u, pairs=(0, 1)):
            c, a = divmod(u, 2)
            node_row, node_col = 2 * (c // 2) + a, 2 * (c % 2)
            if u < 0:
                return
            for pair in pairs:
                nc.scalar.activation(out=out_tiles[u, pair][:], in_=out_tiles[u, pair][:], func=RELU)
                nc.sync.dma_start(
                    out=out[
                        node_row, node_col : node_col + 2, :, :, 2 * pair : 2 * pair + 2, :
                    ].rearrange("e n y b o -> (n y) e (b o)"),
                    in_=out_tiles[u, pair][:].rearrange("p (e w) -> p e w", e=2),
                )

        ctx.enter_context(tc.manual_schedule())
        transpose_x(0)
        regroup_w1(0)
        quantise_x(0)
        b1_bank = psum_a.tile([P, N_MOVING], F32, name="b1_bank", tag="a")
        nc.tensor.transpose(b1_bank[:, 0:P], bias_rows[:].bitcast(F32), ident[:])
        b1_pairs = keep.tile([P, PARITIES * CHILDREN], BF16, name="b1_pairs")
        nc.vector.tensor_copy(out=b1_pairs[:].bitcast(F32), in_=b1_bank[:, 0:CHILDREN])
        b1 = keep.tile([P, PARITIES * CHILDREN], F32, name="b1")
        nc.vector.tensor_copy(out=b1[:], in_=b1_pairs[:])
        quantise_w1(0)
        transpose_x(1)
        level1_block(0, 0)
        regroup_w1(1)
        quantise_x(1)
        transpose_x(2)
        level1_block(0, 1)
        quantise_w1(1)
        quantise_x(2)
        quantise_h(0)
        transpose_x(3)
        level1_block(0, 2)
        quantise_x(3)
        level1_block(1, 0)
        regroup_w2(0)
        level1_block(0, 3)
        level1_block(1, 1)
        quantise_w2(0)
        quantise_h(1)
        regroup_w2(1)
        for u in range(UNITS):
            if u % 2 == 0 and (u + 4) // 2 < CHILDREN:
                regroup_w1((u + 4) // 2)
            regroup_w2(u + 2)
            relu_and_store(u - 1, (0,))
            quantise_h(u + 2)
            quantise_w2(u + 1)
            if u % 2 == 0 and (u + 4) // 2 < CHILDREN:
                quantise_w1((u + 4) // 2)
            half = u + 3
            if half < HALVES:
                level1_block(half // 2, 2 * (half % 2))
            relu_and_store(u - 1, (1,))
            level2(u)
            if half < HALVES:
                level1_block(half // 2, 2 * (half % 2) + 1)
        relu_and_store(UNITS - 1)
